import numpy as np
import ml_dtypes


def mxq(x, axis, fmt="e4m3"):
    dtype, down = {"e4m3": (ml_dtypes.float8_e4m3fn, 7), "e5m2": (ml_dtypes.float8_e5m2, 14)}[fmt]
    v = np.moveaxis(np.asarray(x, np.float32).astype(ml_dtypes.bfloat16).astype(np.float64), axis, -1)
    blocks = v.reshape(v.shape[:-1] + (-1, 32))
    amax = np.abs(blocks).max(-1, keepdims=True)
    byte = np.maximum(np.where(amax > 0, np.frexp(amax)[1] - 1 + 127, 0) - down, 1)
    scale = np.exp2(byte - 127.0)
    codes = (blocks / scale).astype(np.float32).astype(dtype).astype(np.float64)
    return np.moveaxis((codes * scale).reshape(v.shape), -1, axis)


WIDE = False


def mx_kscale(k):
    if not WIDE:
        return np.ones(k)
    levels = np.array([10, -10, 5, -5, 0])
    if k % 512:
        return np.exp2(np.random.permutation(np.resize(levels, k // 32))).repeat(32)
    a = np.empty((k // 512, 16))
    for p in range(k // 512):
        a[p, :8] = np.random.permutation(np.resize(levels, 8))
        for g in range(8):
            far = levels[np.abs(levels - a[p, g]) >= 10]
            a[p, g + 8] = far[np.random.randint(len(far))]
    return np.exp2(a.ravel()).repeat(32)


BF16 = ml_dtypes.bfloat16


def bf(x):
    return np.asarray(x, np.float32).astype(BF16)


def f64(x):
    return np.asarray(x).astype(np.float64)


B, H, W, C, NH = 1, 128, 8, 1024, 8
HD = C // NH
RD = (HD // 2) * 2
HALF = RD // 2
ROPE_MIN_LOG = -12.0
ROPE_MAX_LOG = 0.0
EPS = 1e-6


def rms_norm(h, g):
    var = np.mean(h * h, axis=-1, keepdims=True)
    return g * (h * (1.0 / np.sqrt(var + EPS)))


def rope(t):
    pos = np.linspace(0.0, 1.0, H)
    freqs = np.exp(np.linspace(ROPE_MIN_LOG, ROPE_MAX_LOG, HALF))
    ang = pos[:, None] * freqs[None, :] * H
    cos, sin = np.cos(ang), np.sin(ang)
    rot = t[..., :RD].reshape(B * W, NH, H, HALF, 2)
    te, to = rot[..., 0], rot[..., 1]
    e2 = te * cos - to * sin
    o2 = te * sin + to * cos
    rot2 = np.stack([e2, o2], axis=-1).reshape(B * W, NH, H, RD)
    return np.concatenate([rot2, t[..., RD:]], axis=-1)


def heads(y):
    return y.reshape(B * W, H, NH, HD).transpose(0, 2, 1, 3)


def draw0():
    s = mx_kscale(C)
    return {'x': bf(np.random.standard_normal((B, H, W, C)) * s),
            'w_qkv': bf(np.random.standard_normal((3 * C, C)) / np.sqrt(C) / s[None, :]),
            'q_norm_w': bf(1.0 + 0.1 * np.random.standard_normal(HD)),
            'k_norm_w': bf(1.0 + 0.1 * np.random.standard_normal(HD))}


def core(x, w_qkv, q_norm_w, k_norm_w):
    xr = f64(x).transpose(0, 2, 1, 3).reshape(B * W, H, C)
    xq = mxq(xr, 2, 'e4m3')
    wt = f64(w_qkv).T
    q = heads(xq @ mxq(wt[:, :C], 0, 'e4m3'))
    k = heads(xq @ mxq(wt[:, C:2 * C], 0, 'e4m3'))
    v = heads(xq @ mxq(wt[:, 2 * C:], 0, 'e4m3'))
    q = rope(rms_norm(q, f64(q_norm_w)))
    k = rope(rms_norm(k, f64(k_norm_w)))
    return q, k, v


def e4m3fn_bytes(y):
    return np.clip(np.asarray(y, np.float64), -448.0, 448.0).astype(np.float32).astype(ml_dtypes.float8_e4m3fn).view(np.uint8)


def e4m3fn_values(b):
    return np.asarray(b, np.uint8).view(ml_dtypes.float8_e4m3fn).astype(np.float64)


def setup_inputs():
    d = draw0()
    x0 = np.asarray(d['w_qkv']).astype(np.float64)
    s = (np.max(np.abs(x0), axis=(0,), keepdims=True) / 448.0).astype(np.float32)
    out = {}
    for k, v in d.items():
        if k == 'w_qkv':
            out['w_qkv_bytes'] = e4m3fn_bytes(x0 / s.astype(np.float64))
            out['w_qkv_scale'] = s
        else:
            out[k] = v
    return out


def reference(x, w_qkv_bytes, w_qkv_scale, q_norm_w, k_norm_w):
    return core(x, e4m3fn_values(w_qkv_bytes) * w_qkv_scale.astype(np.float64), q_norm_w, k_norm_w)

@@ -1,0 +1,292 @@
+from contextlib import ExitStack
+
+import concourse.mybir as mybir
+from concourse.masks import make_identity
+
+FLOPS = 2 * 1024 * 1024 * 3072
+
+F32 = mybir.dt.float32
+BF16 = mybir.dt.bfloat16
+U32 = mybir.dt.uint32
+U8 = mybir.dt.uint8
+I32 = mybir.dt.int32
+FP8 = mybir.dt.float8_e4m3fn
+FP8X4 = mybir.dt.float8_e4m3fn_x4
+ALU = mybir.AluOpType
+ACT = mybir.ActivationFunctionType
+
+P = 128
+NW = 8
+C = 1024
+GROUP = 512
+EPS = 1e-6
+PI = 3.141592653589793
+E = 2.718281828459045
+TWO_PI_HI = 6.28125
+TWO_PI_LO = 2.0 * PI - TWO_PI_HI
+ADD_ON_G = True
+PE_FROM = 7
+
+
+def tile_seisdit_pa_kernel(tc, x, w_qkv_bytes, w_qkv_scale, q_norm_w, k_norm_w, out_0, out_1, out_2):
+    nc = tc.nc
+    outs = (out_0, out_1, out_2)
+    order = [4, 5, 0, 1, 2, 3]
+
+    with ExitStack() as ctx:
+        keep = ctx.enter_context(tc.tile_pool(name="keep", bufs=1))
+        work = ctx.enter_context(tc.tile_pool(name="work", bufs=2))
+        tp_pool = ctx.enter_context(tc.psum_pool(name="tpp", bufs=2))
+        acc_pool = ctx.enter_context(tc.psum_pool(name="accp", bufs=6))
+        ctx.enter_context(tc.manual_schedule())
+
+        sc = keep.tile([P, C], F32, name="sc")
+        nc.sync.dma_start(out=sc[:], in_=w_qkv_scale.rearrange("o k -> (o k)").partition_broadcast(P))
+        wb = {}
+
+        def load_w(c, parts):
+            t = keep.tile([P, 4, C], U8, name="wbytes%d" % c)
+            step = 4 // parts
+            for a in range(0, 4, step):
+                rows = w_qkv_bytes[c * GROUP + a * P:c * GROUP + (a + step) * P, :]
+                nc.sync.dma_start(out=t[:, a:a + step, :], in_=rows.rearrange("(a p) k -> p a k", p=P))
+            wb[c] = t
+
+        load_w(order[0], 4)
+        x_sb = []
+        gains = []
+        for i in range(4):
+            t = keep.tile([P, 2, C], BF16, name="x_sb%d" % i)
+            nc.sync.dma_start(out=t[:], in_=x[0, :, 2 * i:2 * i + 2, :])
+            x_sb.append(t)
+        load_w(order[1], 1)
+        for i, gvec in enumerate((q_norm_w, k_norm_w)):
+            t = keep.tile([P, P], BF16, name="gain%d" % i)
+            nc.sync.dma_start(out=t[:], in_=gvec.partition_broadcast(P))
+            gains.append(t)
+        s_kt = keep.tile([P, 8], F32, name="s_kt")
+        nc.sync.dma_start(out=s_kt[:].rearrange("p (g t) -> p g t", t=4),
+                          in_=w_qkv_scale.rearrange("o (g p t) -> p (o g) t", g=2, p=P, t=4))
+        for c in order[2:]:
+            load_w(c, 1)
+
+        h_i = keep.tile([P, 1], I32, name="h_i")
+        nc.gpsimd.iota(h_i[:], pattern=[[0, 1]], base=0, channel_multiplier=1)
+        ident = keep.tile([P, P], F32, name="ident")
+        make_identity(nc, ident[:])
+        h_f = keep.tile([P, 1], F32, name="h_f")
+        nc.vector.tensor_copy(out=h_f[:], in_=h_i[:])
+        fr = keep.tile([P, 64], F32, name="fr")
+        nc.vector.memset(fr[:, 0:1], 1.0)
+        warm = keep.tile([P, 2], F32, name="warm")
+        nc.scalar.activation(out=warm[:, 0:1], in_=fr[:, 0:1], func=ACT.Sin)
+        for b in range(6):
+            n = 1 << b
+            nc.vector.tensor_scalar(out=fr[:, n:2 * n], in0=fr[:, 0:n], scalar1=E ** (12.0 * n / 63.0), scalar2=None, op0=ALU.mult)
+        ang = keep.tile([P, 64], F32, name="ang")
+        nc.vector.tensor_scalar(out=ang[:], in0=fr[:], scalar1=h_f[:, 0:1], scalar2=(128.0 / 127.0) * E ** (-12.0), op0=ALU.mult, op1=ALU.mult)
+        turns_i = keep.tile([P, 64], I32, name="turns_i")
+        nc.vector.tensor_scalar(out=turns_i[:], in0=ang[:], scalar1=1.0 / (2.0 * PI), scalar2=None, op0=ALU.mult)
+        turns = keep.tile([P, 64], F32, name="turns")
+        nc.vector.tensor_copy(out=turns[:], in_=turns_i[:])
+        r1 = keep.tile([P, 64], F32, name="r1")
+        nc.vector.scalar_tensor_tensor(out=r1[:], in0=turns[:], scalar=-TWO_PI_HI, in1=ang[:], op0=ALU.mult, op1=ALU.add)
+        red = keep.tile([P, 64], F32, name="red")
+        nc.vector.scalar_tensor_tensor(out=red[:], in0=turns[:], scalar=-TWO_PI_LO, in1=r1[:], op0=ALU.mult, op1=ALU.add)
+        s4 = keep.tile([P, 64], F32, name="s4")
+        nc.scalar.activation(out=s4[:], in_=red[:], func=ACT.Sin, scale=0.25)
+        s8 = keep.tile([P, 64], F32, name="s8")
+        nc.scalar.activation(out=s8[:], in_=red[:], func=ACT.Sin, scale=0.125)
+        nc.scalar.activation(out=warm[:, 1:2], in_=fr[:, 0:1], func=ACT.Abs_reciprocal_sqrt)
+        tables = []
+
+        def one_minus_twice_square(name, src):
+            sq = keep.tile([P, 64], F32, name=name + "_sq")
+            nc.vector.tensor_tensor(out=sq[:], in0=src[:], in1=src[:], op=ALU.mult)
+            res = keep.tile([P, 64], F32, name=name)
+            nc.vector.tensor_scalar(out=res[:], in0=sq[:], scalar1=-2.0, scalar2=1.0, op0=ALU.mult, op1=ALU.add)
+            return res
+
+        trig = {}
+
+        def build_trig():
+            c4 = one_minus_twice_square("c4", s8)
+            c2 = one_minus_twice_square("c2", s4)
+            s2 = keep.tile([P, 64], F32, name="s2")
+            nc.vector.scalar_tensor_tensor(out=s2[:], in0=s4[:], scalar=2.0, in1=c4[:], op0=ALU.mult, op1=ALU.mult)
+            cosr = one_minus_twice_square("cosr", s2)
+            pm_sin = keep.tile([P, 64, 2], F32, name="pm_sin")
+            nc.vector.scalar_tensor_tensor(out=pm_sin[:, :, 0], in0=s2[:], scalar=2.0, in1=c2[:], op0=ALU.mult, op1=ALU.mult)
+            nc.vector.scalar_tensor_tensor(out=pm_sin[:, :, 1], in0=s2[:], scalar=-2.0, in1=c2[:], op0=ALU.mult, op1=ALU.mult)
+            trig["cos"] = cosr
+            trig["pm_sin"] = pm_sin
+
+        def build_tables():
+            cosr = trig["cos"]
+            pm_sin = trig["pm_sin"]
+            for i in range(2):
+                t = keep.tile([P, 2, P], F32, name="table%d" % i)
+                gv = gains[i][:].rearrange("p (j e) -> p j e", e=2)
+                nc.vector.tensor_tensor(out=t[:, 0, :].rearrange("p (j e) -> p j e", e=2), in0=gv, in1=cosr[:].unsqueeze(2).to_broadcast([P, 64, 2]), op=ALU.mult)
+                nc.vector.tensor_tensor(out=t[:, 1, :].rearrange("p (j e) -> p j e", e=2), in0=gv, in1=pm_sin[:], op=ALU.mult)
+                tables.append(t)
+
+        def turn_only(words):
+            tp = tp_pool.tile([P, 2, 2, P], F32, name="tp", tag="tp")
+            for g in range(2):
+                for u in range(2):
+                    nc.tensor.transpose(tp[:, g, u, :], words[:, 256 * g + u:256 * (g + 1):2], ident[:])
+            return tp
+
+        def turn(words, dst):
+            tp = turn_only(words)
+            nc.scalar.copy(out=dst, in_=tp[:].rearrange("p g u r -> p g r u"))
+
+        late_bf = {}
+        late_tp = {}
+
+        def late_widen(c, a):
+            late_bf[(c, a)] = work.tile([P, C], BF16, name="lbf", tag="lbf", bufs=8)
+            nc.scalar.copy(out=late_bf[(c, a)][:], in_=wb[c][:, a, :].bitcast(FP8))
+
+        def late_turn(c, a):
+            late_tp[(c, a)] = turn_only(late_bf[(c, a)][:].bitcast(F32))
+
+        def late_scale(c, a):
+            if a == 0:
+                gw_of[c] = work.tile([P, 4096], BF16, name="gw", tag="gw", bufs=3, align_bytes=64)
+            for g in range(2):
+                nc.vector.tensor_tensor(
+                    out=gw_of[c][:, g * 2048 + a * 512:g * 2048 + (a + 1) * 512].rearrange("p (r u e) -> p r u e", u=2, e=2),
+                    in0=late_tp[(c, a)][:, g].rearrange("p u r -> p (u r)").bitcast(BF16).rearrange("p (u r e) -> p r u e", u=2, e=2),
+                    in1=s_kt[:, 4 * g:4 * g + 4].rearrange("p (u e) -> p u e", e=2).unsqueeze(1).to_broadcast([P, P, 2, 2]),
+                    op=ALU.mult)
+
+        gw_of = {}
+        wc = {}
+        ws = {}
+
+        def widen_and_turn(c, a):
+            if a == 0:
+                gw_of[c] = work.tile([P, 4096], BF16, name="gw", tag="gw", bufs=3, align_bytes=64)
+            wbf = work.tile([P, C], BF16, name="wbf", tag="wbf", bufs=5)
+            nc.vector.tensor_tensor(out=wbf[:], in0=wb[c][:, a, :].bitcast(FP8), in1=sc[:], op=ALU.mult)
+            dst = gw_of[c][:].bitcast(F32).rearrange("p (g r u) -> p g r u", g=2, u=2)[:, :, a * P:(a + 1) * P, :]
+            turn(wbf[:].bitcast(F32), dst)
+
+        def quantize_w(c):
+            wc[c] = keep.tile([P, 2, GROUP], U32, name="wc%d" % c, align_bytes=64)
+            ws[c] = keep.tile([P, 2, GROUP], U8, name="ws%d" % c, align_bytes=64)
+            nc.vector.quantize_mx(out=wc[c][:].rearrange("p g r -> p (g r)").bitcast(FP8X4), scales=ws[c][:].rearrange("p g r -> p (g r)"), in_=gw_of[c][:])
+
+        xg_of = {}
+        xc = {}
+        xs = {}
+
+        def turn_x(i):
+            xg_of[i] = work.tile([P, 2 * C], BF16, name="xg", tag="xg", bufs=4, align_bytes=64)
+            for b in range(2):
+                turn(x_sb[i][:, b, :].bitcast(F32), xg_of[i][:, b * C:(b + 1) * C].bitcast(F32).rearrange("p (g r u) -> p g r u", g=2, u=2))
+
+        def quantize_x(i):
+            codes = keep.tile([P, 512], U32, name="xc%d" % i, align_bytes=64)
+            planes = keep.tile([P, 512], U8, name="xs%d" % i, align_bytes=64)
+            nc.vector.quantize_mx(out=codes[:].bitcast(FP8X4), scales=planes[:], in_=xg_of[i][:])
+            for b in range(2):
+                xc[2 * i + b] = codes[:, b * 256:(b + 1) * 256]
+                xs[2 * i + b] = planes[:, b * 256:(b + 1) * 256]
+
+        def product(c, w, late=False):
+            if late:
+                acc = tp_pool.tile([P, GROUP], F32, name="tp", tag="tp")
+            else:
+                acc = acc_pool.tile([P, GROUP], F32, name="acc", tag="acc")
+            for g in range(2):
+                cols = slice(g * P, (g + 1) * P)
+                nc.tensor.matmul_mx(out=acc[:], lhsT=xc[w][:, cols].bitcast(FP8X4), lhsT_scale=xs[w][:, cols],
+                                    rhs=wc[c][:, g, :].bitcast(FP8X4), rhs_scale=ws[c][:, g, :],
+                                    start=(g == 0), stop=(g == 1))
+            return acc
+
+        def value_bank(c, w, late=False):
+            acc = product(c, w, late)
+            ov = work.tile([P, 4, P], F32, name="ov", tag="ov", bufs=3)
+            nc.scalar.copy(out=ov[:].rearrange("p n d -> p (n d)"), in_=acc[:])
+            n0 = 4 * (c % 2)
+            nc.sync.dma_start(out=outs[2][w, n0:n0 + 4].rearrange("n h d -> h n d"), in_=ov[:])
+
+        accs = {}
+        rstds = {}
+
+        def unit_head(u):
+            which, w = u // NW, u % NW
+            accs[u] = [product(2 * which + b, w) for b in range(2)]
+            ss = work.tile([P, 8], F32, name="ss", tag="ss", bufs=4)
+            for n in range(8):
+                junk = work.tile([P, P], BF16, name="junk", tag="junk", bufs=2)
+                nc.scalar.activation(out=junk[:], in_=accs[u][n // 4][:, (n % 4) * P:(n % 4 + 1) * P], func=ACT.Square, accum_out=ss[:, n:n + 1])
+            rstds[u] = work.tile([P, 8], F32, name="rstd", tag="rstd", bufs=4)
+            nc.scalar.activation(out=rstds[u][:], in_=ss[:], func=ACT.Abs_reciprocal_sqrt, scale=1.0 / 128.0, bias=EPS)
+
+        def unit_tail(u, pieces, before_last=None):
+            which, w = u // NW, u % NW
+            tt = work.tile([P, 2, 8, P], F32, name="tt", tag="tt", bufs=3)
+            o = work.tile([P, 8, P], F32, name="o", tag="o", bufs=3)
+            eng = nc.gpsimd if ADD_ON_G else nc.vector
+            def rope_products(n):
+                nc.vector.scalar_tensor_tensor(out=tt[:, :, n, :], in0=accs[u][n // 4][:, (n % 4) * P:(n % 4 + 1) * P].unsqueeze(1).to_broadcast([P, 2, P]),
+                                               scalar=rstds[u][:, n:n + 1], in1=tables[which][:], op0=ALU.mult, op1=ALU.mult)
+
+            for n in range(PE_FROM, 8):
+                rope_products(n)
+            pa = tp_pool.tile([P, (8 - PE_FROM) * P], F32, name="tp", tag="tp")
+            nc.tensor.matmul(out=pa[:], lhsT=ident[:], rhs=tt[:, 0, PE_FROM:8].rearrange("p n d -> p (n d)"), start=True, stop=False)
+            nc.tensor.matmul(out=pa[:].rearrange("p (m e) -> p m e", e=2), lhsT=ident[:],
+                             rhs=tt[:, 1, PE_FROM:8].rearrange("p n (j e) -> p (n j) e", e=2)[:, :, ::-1], start=False, stop=True)
+            nc.scalar.copy(out=o[:, PE_FROM:8].rearrange("p n d -> p (n d)"), in_=pa[:])
+            cuts = [0, PE_FROM] if pieces == 1 else [0, 4, PE_FROM]
+            for n0, n1 in zip(cuts[:-1], cuts[1:]):
+                for n in range(n0, n1):
+                    if n == PE_FROM - 1 and before_last is not None:
+                        before_last()
+                    rope_products(n)
+                eng.tensor_tensor(out=o[:, n0:n1].rearrange("p n (j e) -> p (n j) e", e=2),
+                                  in0=tt[:, 0, n0:n1].rearrange("p n (j e) -> p (n j) e", e=2),
+                                  in1=tt[:, 1, n0:n1].rearrange("p n (j e) -> p (n j) e", e=2)[:, :, ::-1], op=ALU.add)
+                if pieces > 1:
+                    nc.sync.dma_start(out=outs[which][w, n0:n1].rearrange("n h d -> h n d"), in_=o[:, n0:n1])
+            if pieces > 1:
+                nc.sync.dma_start(out=outs[which][w, PE_FROM:8].rearrange("n h d -> h n d"), in_=o[:, PE_FROM:8])
+            else:
+                nc.sync.dma_start(out=outs[which][w].rearrange("n h d -> h n d"), in_=o[:])
+
+        tiles = [(c, a) for c in order for a in range(4)]
+        values = [(c, w) for c in (4, 5) for w in range(NW)]
+        nv = 0
+        for t, (c, a) in enumerate(tiles):
+            widen_and_turn(c, a)
+            if t < 4:
+                turn_x(t)
+            if t == 1:
+                build_trig()
+            if 3 <= t < 7:
+                quantize_x(t - 3)
+            if t == 7:
+                build_tables()
+            if a == 1 and t > 1:
+                quantize_w(tiles[t - 2][0])
+            if t >= 7 and t % 2 == 1 and nv < len(values):
+                value_bank(*values[nv])
+                value_bank(*values[nv + 1])
+                nv += 2
+        unit_head(0)
+        unit_head(1)
+        unit_head(2)
+
+        for u in range(2 * NW):
+            if u == 0:
+                unit_tail(u, 1, lambda: quantize_w(order[-1]))
+            else:
+                unit_tail(u, 1 if u < 2 * NW - 1 else 2)
+            if u + 3 < 2 * NW:
+                unit_head(u + 3)

@@ -26,6 +26,7 @@ TWO_PI_HI = 6.28125
 TWO_PI_LO = 2.0 * PI - TWO_PI_HI
 ADD_ON_G = True
 PE_FROM = 7
+PE_FROM_END = 5
 
 
 def tile_seisdit_pa_kernel(tc, x, w_qkv_bytes, w_qkv_scale, q_norm_w, k_norm_w, out_0, out_1, out_2):
@@ -74,8 +75,6 @@ def tile_seisdit_pa_kernel(tc, x, w_qkv_bytes, w_qkv_scale, q_norm_w, k_norm_w, 
         nc.gpsimd.iota(h_i[:], pattern=[[0, 1]], base=0, channel_multiplier=1)
         ident = keep.tile([P, P], F32, name="ident")
         make_identity(nc, ident[:])
-        h_f = keep.tile([P, 1], F32, name="h_f")
-        nc.vector.tensor_copy(out=h_f[:], in_=h_i[:])
         fr = keep.tile([P, 64], F32, name="fr")
         nc.vector.memset(fr[:, 0:1], 1.0)
         warm = keep.tile([P, 2], F32, name="warm")
@@ -83,6 +82,8 @@ def tile_seisdit_pa_kernel(tc, x, w_qkv_bytes, w_qkv_scale, q_norm_w, k_norm_w, 
         for b in range(6):
             n = 1 << b
             nc.vector.tensor_scalar(out=fr[:, n:2 * n], in0=fr[:, 0:n], scalar1=E ** (12.0 * n / 63.0), scalar2=None, op0=ALU.mult)
+        h_f = keep.tile([P, 1], F32, name="h_f")
+        nc.vector.tensor_copy(out=h_f[:], in_=h_i[:])
         ang = keep.tile([P, 64], F32, name="ang")
         nc.vector.tensor_scalar(out=ang[:], in0=fr[:], scalar1=h_f[:, 0:1], scalar2=(128.0 / 127.0) * E ** (-12.0), op0=ALU.mult, op1=ALU.mult)
         turns_i = keep.tile([P, 64], I32, name="turns_i")
@@ -183,10 +184,10 @@ def tile_seisdit_pa_kernel(tc, x, w_qkv_bytes, w_qkv_scale, q_norm_w, k_norm_w, 
         xc = {}
         xs = {}
 
-        def turn_x(i):
-            xg_of[i] = work.tile([P, 2 * C], BF16, name="xg", tag="xg", bufs=4, align_bytes=64)
-            for b in range(2):
-                turn(x_sb[i][:, b, :].bitcast(F32), xg_of[i][:, b * C:(b + 1) * C].bitcast(F32).rearrange("p (g r u) -> p g r u", g=2, u=2))
+        def turn_x(i, b):
+            if b == 0:
+                xg_of[i] = work.tile([P, 2 * C], BF16, name="xg", tag="xg", bufs=4, align_bytes=64)
+            turn(x_sb[i][:, b, :].bitcast(F32), xg_of[i][:, b * C:(b + 1) * C].bitcast(F32).rearrange("p (g r u) -> p g r u", g=2, u=2))
 
         def quantize_x(i):
             codes = keep.tile([P, 512], U32, name="xc%d" % i, align_bytes=64)
@@ -228,7 +229,7 @@ def tile_seisdit_pa_kernel(tc, x, w_qkv_bytes, w_qkv_scale, q_norm_w, k_norm_w, 
             rstds[u] = work.tile([P, 8], F32, name="rstd", tag="rstd", bufs=4)
             nc.scalar.activation(out=rstds[u][:], in_=ss[:], func=ACT.Abs_reciprocal_sqrt, scale=1.0 / 128.0, bias=EPS)
 
-        def unit_tail(u, pieces, before_last=None):
+        def unit_tail(u, pe_from, cuts, before_last=None):
             which, w = u // NW, u % NW
             tt = work.tile([P, 2, 8, P], F32, name="tt", tag="tt", bufs=3)
             o = work.tile([P, 8, P], F32, name="o", tag="o", bufs=3)
@@ -237,17 +238,17 @@ def tile_seisdit_pa_kernel(tc, x, w_qkv_bytes, w_qkv_scale, q_norm_w, k_norm_w, 
                 nc.vector.scalar_tensor_tensor(out=tt[:, :, n, :], in0=accs[u][n // 4][:, (n % 4) * P:(n % 4 + 1) * P].unsqueeze(1).to_broadcast([P, 2, P]),
                                                scalar=rstds[u][:, n:n + 1], in1=tables[which][:], op0=ALU.mult, op1=ALU.mult)
 
-            for n in range(PE_FROM, 8):
+            pieces = len(cuts) - 1
+            for n in range(pe_from, 8):
                 rope_products(n)
-            pa = tp_pool.tile([P, (8 - PE_FROM) * P], F32, name="tp", tag="tp")
-            nc.tensor.matmul(out=pa[:], lhsT=ident[:], rhs=tt[:, 0, PE_FROM:8].rearrange("p n d -> p (n d)"), start=True, stop=False)
+            pa = tp_pool.tile([P, (8 - pe_from) * P], F32, name="tp", tag="tp")
+            nc.tensor.matmul(out=pa[:], lhsT=ident[:], rhs=tt[:, 0, pe_from:8].rearrange("p n d -> p (n d)"), start=True, stop=False)
             nc.tensor.matmul(out=pa[:].rearrange("p (m e) -> p m e", e=2), lhsT=ident[:],
-                             rhs=tt[:, 1, PE_FROM:8].rearrange("p n (j e) -> p (n j) e", e=2)[:, :, ::-1], start=False, stop=True)
-            nc.scalar.copy(out=o[:, PE_FROM:8].rearrange("p n d -> p (n d)"), in_=pa[:])
-            cuts = [0, PE_FROM] if pieces == 1 else [0, 4, PE_FROM]
+                             rhs=tt[:, 1, pe_from:8].rearrange("p n (j e) -> p (n j) e", e=2)[:, :, ::-1], start=False, stop=True)
+            nc.scalar.copy(out=o[:, pe_from:8].rearrange("p n d -> p (n d)"), in_=pa[:])
             for n0, n1 in zip(cuts[:-1], cuts[1:]):
                 for n in range(n0, n1):
-                    if n == PE_FROM - 1 and before_last is not None:
+                    if n == pe_from - 1 and before_last is not None:
                         before_last()
                     rope_products(n)
                 eng.tensor_tensor(out=o[:, n0:n1].rearrange("p n (j e) -> p (n j) e", e=2),
@@ -255,38 +256,41 @@ def tile_seisdit_pa_kernel(tc, x, w_qkv_bytes, w_qkv_scale, q_norm_w, k_norm_w, 
                                   in1=tt[:, 1, n0:n1].rearrange("p n (j e) -> p (n j) e", e=2)[:, :, ::-1], op=ALU.add)
                 if pieces > 1:
                     nc.sync.dma_start(out=outs[which][w, n0:n1].rearrange("n h d -> h n d"), in_=o[:, n0:n1])
-            if pieces > 1:
-                nc.sync.dma_start(out=outs[which][w, PE_FROM:8].rearrange("n h d -> h n d"), in_=o[:, PE_FROM:8])
-            else:
+                    if n0 == 0:
+                        nc.sync.dma_start(out=outs[which][w, pe_from:8].rearrange("n h d -> h n d"), in_=o[:, pe_from:8])
+            if pieces == 1:
                 nc.sync.dma_start(out=outs[which][w].rearrange("n h d -> h n d"), in_=o[:])
 
         tiles = [(c, a) for c in order for a in range(4)]
         values = [(c, w) for c in (4, 5) for w in range(NW)]
         nv = 0
+        build_trig()
         for t, (c, a) in enumerate(tiles):
             widen_and_turn(c, a)
-            if t < 4:
-                turn_x(t)
-            if t == 1:
-                build_trig()
-            if 3 <= t < 7:
-                quantize_x(t - 3)
-            if t == 7:
+            if t < 8:
+                turn_x(t // 2, t % 2)
+            if t in (5, 7, 9, 11):
+                quantize_x((t - 5) // 2)
+            if t == 8:
                 build_tables()
-            if a == 1 and t > 1:
-                quantize_w(tiles[t - 2][0])
+            if a == 2 and t > 2:
+                quantize_w(tiles[t - 3][0])
             if t >= 7 and t % 2 == 1 and nv < len(values):
                 value_bank(*values[nv])
                 value_bank(*values[nv + 1])
                 nv += 2
-        unit_head(0)
-        unit_head(1)
+            if t >= len(tiles) - 2:
+                unit_head(t - (len(tiles) - 2))
         unit_head(2)
 
         for u in range(2 * NW):
             if u == 0:
-                unit_tail(u, 1, lambda: quantize_w(order[-1]))
+                unit_tail(u, PE_FROM, [0, PE_FROM], lambda: quantize_w(order[-1]))
+            elif u + 3 < 2 * NW:
+                unit_tail(u, PE_FROM, [0, PE_FROM])
+            elif u < 2 * NW - 1:
+                unit_tail(u, PE_FROM_END, [0, PE_FROM_END])
             else:
-                unit_tail(u, 1 if u < 2 * NW - 1 else 2)
+                unit_tail(u, PE_FROM_END, [0, 3, PE_FROM_END])
             if u + 3 < 2 * NW:
                 unit_head(u + 3)

@@ -44,32 +44,33 @@ def tile_seisdit_pa_kernel(tc, x, w_qkv_bytes, w_qkv_scale, q_norm_w, k_norm_w, 
         sc = keep.tile([P, C], F32, name="sc")
         nc.sync.dma_start(out=sc[:], in_=w_qkv_scale.rearrange("o k -> (o k)").partition_broadcast(P))
         wb = {}
-
-        def load_w(c, parts):
-            t = keep.tile([P, 4, C], U8, name="wbytes%d" % c)
-            step = 4 // parts
-            for a in range(0, 4, step):
-                rows = w_qkv_bytes[c * GROUP + a * P:c * GROUP + (a + step) * P, :]
-                nc.sync.dma_start(out=t[:, a:a + step, :], in_=rows.rearrange("(a p) k -> p a k", p=P))
-            wb[c] = t
-
-        load_w(order[0], 4)
+        for c in order:
+            wb[c] = keep.tile([P, 4, C], U8, name="wbytes%d" % c)
         x_sb = []
-        gains = []
         for i in range(4):
-            t = keep.tile([P, 2, C], BF16, name="x_sb%d" % i)
-            nc.sync.dma_start(out=t[:], in_=x[0, :, 2 * i:2 * i + 2, :])
-            x_sb.append(t)
-        load_w(order[1], 1)
+            x_sb.append(keep.tile([P, 2, C], BF16, name="x_sb%d" % i))
+
+        def load_w(c, a0, a1):
+            rows = w_qkv_bytes[c * GROUP + a0 * P:c * GROUP + a1 * P, :]
+            nc.sync.dma_start(out=wb[c][:, a0:a1, :], in_=rows.rearrange("(a p) k -> p a k", p=P))
+
+        def load_x(i):
+            nc.sync.dma_start(out=x_sb[i][:], in_=x[0, :, 2 * i:2 * i + 2, :])
+
+        load_w(order[0], 0, 1)
+        load_w(order[0], 1, 2)
+        load_x(0)
+        load_w(order[0], 2, 4)
+        load_x(1)
+        load_w(order[1], 0, 2)
+        load_x(2)
+        load_w(order[1], 2, 4)
+        load_x(3)
+        gains = keep.tile([P, 2, P], BF16, name="gains")
         for i, gvec in enumerate((q_norm_w, k_norm_w)):
-            t = keep.tile([P, P], BF16, name="gain%d" % i)
-            nc.sync.dma_start(out=t[:], in_=gvec.partition_broadcast(P))
-            gains.append(t)
-        s_kt = keep.tile([P, 8], F32, name="s_kt")
-        nc.sync.dma_start(out=s_kt[:].rearrange("p (g t) -> p g t", t=4),
-                          in_=w_qkv_scale.rearrange("o (g p t) -> p (o g) t", g=2, p=P, t=4))
+            nc.sync.dma_start(out=gains[:, i, :], in_=gvec.partition_broadcast(P))
         for c in order[2:]:
-            load_w(c, 1)
+            load_w(c, 0, 4)
 
         h_i = keep.tile([P, 1], I32, name="h_i")
         nc.gpsimd.iota(h_i[:], pattern=[[0, 1]], base=0, channel_multiplier=1)
@@ -94,43 +95,25 @@ def tile_seisdit_pa_kernel(tc, x, w_qkv_bytes, w_qkv_scale, q_norm_w, k_norm_w, 
         nc.vector.scalar_tensor_tensor(out=r1[:], in0=turns[:], scalar=-TWO_PI_HI, in1=ang[:], op0=ALU.mult, op1=ALU.add)
         red = keep.tile([P, 64], F32, name="red")
         nc.vector.scalar_tensor_tensor(out=red[:], in0=turns[:], scalar=-TWO_PI_LO, in1=r1[:], op0=ALU.mult, op1=ALU.add)
-        s4 = keep.tile([P, 64], F32, name="s4")
-        nc.scalar.activation(out=s4[:], in_=red[:], func=ACT.Sin, scale=0.25)
-        s8 = keep.tile([P, 64], F32, name="s8")
-        nc.scalar.activation(out=s8[:], in_=red[:], func=ACT.Sin, scale=0.125)
+        sh = keep.tile([P, 64], F32, name="sh")
+        nc.scalar.activation(out=sh[:], in_=red[:], func=ACT.Sin, scale=0.5)
+        ab = keep.tile([P, 64], F32, name="ab")
+        nc.scalar.activation(out=ab[:], in_=red[:], func=ACT.Abs)
+        ch = keep.tile([P, 64], F32, name="ch")
+        nc.scalar.activation(out=ch[:], in_=ab[:], func=ACT.Sin, scale=-0.5, bias=PI / 2.0)
+        sq = keep.tile([P, 64], F32, name="sq")
+        nc.scalar.activation(out=sq[:], in_=sh[:], func=ACT.Square)
+        trig = keep.tile([P, 2, 64, 2], F32, name="trig")
+        nc.scalar.activation(out=trig[:, 0], in_=sq[:].unsqueeze(2).to_broadcast([P, 64, 2]), func=ACT.Copy, scale=-2.0, bias=1.0)
         nc.scalar.activation(out=warm[:, 1:2], in_=fr[:, 0:1], func=ACT.Abs_reciprocal_sqrt)
-        tables = []
-
-        def one_minus_twice_square(name, src):
-            sq = keep.tile([P, 64], F32, name=name + "_sq")
-            nc.vector.tensor_tensor(out=sq[:], in0=src[:], in1=src[:], op=ALU.mult)
-            res = keep.tile([P, 64], F32, name=name)
-            nc.vector.tensor_scalar(out=res[:], in0=sq[:], scalar1=-2.0, scalar2=1.0, op0=ALU.mult, op1=ALU.add)
-            return res
-
-        trig = {}
-
-        def build_trig():
-            c4 = one_minus_twice_square("c4", s8)
-            c2 = one_minus_twice_square("c2", s4)
-            s2 = keep.tile([P, 64], F32, name="s2")
-            nc.vector.scalar_tensor_tensor(out=s2[:], in0=s4[:], scalar=2.0, in1=c4[:], op0=ALU.mult, op1=ALU.mult)
-            cosr = one_minus_twice_square("cosr", s2)
-            pm_sin = keep.tile([P, 64, 2], F32, name="pm_sin")
-            nc.vector.scalar_tensor_tensor(out=pm_sin[:, :, 0], in0=s2[:], scalar=2.0, in1=c2[:], op0=ALU.mult, op1=ALU.mult)
-            nc.vector.scalar_tensor_tensor(out=pm_sin[:, :, 1], in0=s2[:], scalar=-2.0, in1=c2[:], op0=ALU.mult, op1=ALU.mult)
-            trig["cos"] = cosr
-            trig["pm_sin"] = pm_sin
+        tables_all = keep.tile([P, 2, 2, P], F32, name="tables")
+        tables = [tables_all[:, 0], tables_all[:, 1]]
 
         def build_tables():
-            cosr = trig["cos"]
-            pm_sin = trig["pm_sin"]
-            for i in range(2):
-                t = keep.tile([P, 2, P], F32, name="table%d" % i)
-                gv = gains[i][:].rearrange("p (j e) -> p j e", e=2)
-                nc.vector.tensor_tensor(out=t[:, 0, :].rearrange("p (j e) -> p j e", e=2), in0=gv, in1=cosr[:].unsqueeze(2).to_broadcast([P, 64, 2]), op=ALU.mult)
-                nc.vector.tensor_tensor(out=t[:, 1, :].rearrange("p (j e) -> p j e", e=2), in0=gv, in1=pm_sin[:], op=ALU.mult)
-                tables.append(t)
+            nc.vector.scalar_tensor_tensor(out=trig[:, 1, :, 0], in0=sh[:], scalar=2.0, in1=ch[:], op0=ALU.mult, op1=ALU.mult)
+            nc.vector.scalar_tensor_tensor(out=trig[:, 1, :, 1], in0=sh[:], scalar=-2.0, in1=ch[:], op0=ALU.mult, op1=ALU.mult)
+            nc.vector.tensor_tensor(out=tables_all[:], in0=gains[:].unsqueeze(2).to_broadcast([P, 2, 2, P]),
+                                    in1=trig[:].rearrange("p a j e -> p a (j e)").unsqueeze(1).to_broadcast([P, 2, 2, P]), op=ALU.mult)
 
         def turn_only(words):
             tp = tp_pool.tile([P, 2, 2, P], F32, name="tp", tag="tp")
@@ -142,26 +125,6 @@ def tile_seisdit_pa_kernel(tc, x, w_qkv_bytes, w_qkv_scale, q_norm_w, k_norm_w, 
         def turn(words, dst):
             tp = turn_only(words)
             nc.scalar.copy(out=dst, in_=tp[:].rearrange("p g u r -> p g r u"))
-
-        late_bf = {}
-        late_tp = {}
-
-        def late_widen(c, a):
-            late_bf[(c, a)] = work.tile([P, C], BF16, name="lbf", tag="lbf", bufs=8)
-            nc.scalar.copy(out=late_bf[(c, a)][:], in_=wb[c][:, a, :].bitcast(FP8))
-
-        def late_turn(c, a):
-            late_tp[(c, a)] = turn_only(late_bf[(c, a)][:].bitcast(F32))
-
-        def late_scale(c, a):
-            if a == 0:
-                gw_of[c] = work.tile([P, 4096], BF16, name="gw", tag="gw", bufs=3, align_bytes=64)
-            for g in range(2):
-                nc.vector.tensor_tensor(
-                    out=gw_of[c][:, g * 2048 + a * 512:g * 2048 + (a + 1) * 512].rearrange("p (r u e) -> p r u e", u=2, e=2),
-                    in0=late_tp[(c, a)][:, g].rearrange("p u r -> p (u r)").bitcast(BF16).rearrange("p (u r e) -> p r u e", u=2, e=2),
-                    in1=s_kt[:, 4 * g:4 * g + 4].rearrange("p (u e) -> p u e", e=2).unsqueeze(1).to_broadcast([P, P, 2, 2]),
-                    op=ALU.mult)
 
         gw_of = {}
         wc = {}
@@ -236,7 +199,7 @@ def tile_seisdit_pa_kernel(tc, x, w_qkv_bytes, w_qkv_scale, q_norm_w, k_norm_w, 
             eng = nc.gpsimd if ADD_ON_G else nc.vector
             def rope_products(n):
                 nc.vector.scalar_tensor_tensor(out=tt[:, :, n, :], in0=accs[u][n // 4][:, (n % 4) * P:(n % 4 + 1) * P].unsqueeze(1).to_broadcast([P, 2, P]),
-                                               scalar=rstds[u][:, n:n + 1], in1=tables[which][:], op0=ALU.mult, op1=ALU.mult)
+                                               scalar=rstds[u][:, n:n + 1], in1=tables[which], op0=ALU.mult, op1=ALU.mult)
 
             pieces = len(cuts) - 1
             for n in range(pe_from, 8):
@@ -264,7 +227,6 @@ def tile_seisdit_pa_kernel(tc, x, w_qkv_bytes, w_qkv_scale, q_norm_w, k_norm_w, 
         tiles = [(c, a) for c in order for a in range(4)]
         values = [(c, w) for c in (4, 5) for w in range(NW)]
         nv = 0
-        build_trig()
         for t, (c, a) in enumerate(tiles):
             widen_and_turn(c, a)
             if t < 8:
@@ -291,6 +253,6 @@ def tile_seisdit_pa_kernel(tc, x, w_qkv_bytes, w_qkv_scale, q_norm_w, k_norm_w, 
             elif u < 2 * NW - 1:
                 unit_tail(u, PE_FROM_END, [0, PE_FROM_END])
             else:
-                unit_tail(u, PE_FROM_END, [0, 3, PE_FROM_END])
+                unit_tail(u, PE_FROM_END, [0, 2, 4, PE_FROM_END])
             if u + 3 < 2 * NW:
                 unit_head(u + 3)

@@ -24,7 +24,6 @@ PI = 3.141592653589793
 E = 2.718281828459045
 TWO_PI_HI = 6.28125
 TWO_PI_LO = 2.0 * PI - TWO_PI_HI
-ADD_ON_G = True
 PE_FROM = 7
 PE_FROM_END = 5
 
@@ -37,8 +36,7 @@ def tile_seisdit_pa_kernel(tc, x, w_qkv_bytes, w_qkv_scale, q_norm_w, k_norm_w, 
     with ExitStack() as ctx:
         keep = ctx.enter_context(tc.tile_pool(name="keep", bufs=1))
         work = ctx.enter_context(tc.tile_pool(name="work", bufs=2))
-        tp_pool = ctx.enter_context(tc.psum_pool(name="tpp", bufs=2))
-        acc_pool = ctx.enter_context(tc.psum_pool(name="accp", bufs=6))
+        banks = ctx.enter_context(tc.psum_pool(name="banks", bufs=8))
         ctx.enter_context(tc.manual_schedule())
 
         sc = keep.tile([P, C], F32, name="sc")
@@ -116,7 +114,7 @@ def tile_seisdit_pa_kernel(tc, x, w_qkv_bytes, w_qkv_scale, q_norm_w, k_norm_w, 
                                     in1=trig[:].rearrange("p a j e -> p a (j e)").unsqueeze(1).to_broadcast([P, 2, 2, P]), op=ALU.mult)
 
         def turn_only(words):
-            tp = tp_pool.tile([P, 2, 2, P], F32, name="tp", tag="tp")
+            tp = banks.tile([P, 2, 2, P], F32, name="bank", tag="bank")
             for g in range(2):
                 for u in range(2):
                     nc.tensor.transpose(tp[:, g, u, :], words[:, 256 * g + u:256 * (g + 1):2], ident[:])
@@ -132,8 +130,8 @@ def tile_seisdit_pa_kernel(tc, x, w_qkv_bytes, w_qkv_scale, q_norm_w, k_norm_w, 
 
         def widen_and_turn(c, a):
             if a == 0:
-                gw_of[c] = work.tile([P, 4096], BF16, name="gw", tag="gw", bufs=3, align_bytes=64)
-            wbf = work.tile([P, C], BF16, name="wbf", tag="wbf", bufs=5)
+                gw_of[c] = work.tile([P, 4096], BF16, name="gw", tag="gw", bufs=4, align_bytes=64)
+            wbf = work.tile([P, C], BF16, name="wbf", tag="wbf", bufs=8)
             nc.vector.tensor_tensor(out=wbf[:], in0=wb[c][:, a, :].bitcast(FP8), in1=sc[:], op=ALU.mult)
             dst = gw_of[c][:].bitcast(F32).rearrange("p (g r u) -> p g r u", g=2, u=2)[:, :, a * P:(a + 1) * P, :]
             turn(wbf[:].bitcast(F32), dst)
@@ -162,9 +160,9 @@ def tile_seisdit_pa_kernel(tc, x, w_qkv_bytes, w_qkv_scale, q_norm_w, k_norm_w, 
 
         def product(c, w, late=False):
             if late:
-                acc = tp_pool.tile([P, GROUP], F32, name="tp", tag="tp")
+                acc = banks.tile([P, GROUP], F32, name="bank", tag="bank")
             else:
-                acc = acc_pool.tile([P, GROUP], F32, name="acc", tag="acc")
+                acc = banks.tile([P, GROUP], F32, name="bank", tag="bank")
             for g in range(2):
                 cols = slice(g * P, (g + 1) * P)
                 nc.tensor.matmul_mx(out=acc[:], lhsT=xc[w][:, cols].bitcast(FP8X4), lhsT_scale=xs[w][:, cols],
@@ -174,7 +172,7 @@ def tile_seisdit_pa_kernel(tc, x, w_qkv_bytes, w_qkv_scale, q_norm_w, k_norm_w, 
 
         def value_bank(c, w, late=False):
             acc = product(c, w, late)
-            ov = work.tile([P, 4, P], F32, name="ov", tag="ov", bufs=3)
+            ov = work.tile([P, 4, P], F32, name="ov", tag="ov", bufs=6)
             nc.scalar.copy(out=ov[:].rearrange("p n d -> p (n d)"), in_=acc[:])
             n0 = 4 * (c % 2)
             nc.sync.dma_start(out=outs[2][w, n0:n0 + 4].rearrange("n h d -> h n d"), in_=ov[:])
@@ -192,36 +190,36 @@ def tile_seisdit_pa_kernel(tc, x, w_qkv_bytes, w_qkv_scale, q_norm_w, k_norm_w, 
             rstds[u] = work.tile([P, 8], F32, name="rstd", tag="rstd", bufs=4)
             nc.scalar.activation(out=rstds[u][:], in_=ss[:], func=ACT.Abs_reciprocal_sqrt, scale=1.0 / 128.0, bias=EPS)
 
-        def unit_tail(u, pe_from, cuts, before_last=None):
+        def unit_tail(u, pe_from, cuts, before_last=None, own_from=8, store_each=False):
             which, w = u // NW, u % NW
-            tt = work.tile([P, 2, 8, P], F32, name="tt", tag="tt", bufs=3)
-            o = work.tile([P, 8, P], F32, name="o", tag="o", bufs=3)
-            eng = nc.gpsimd if ADD_ON_G else nc.vector
+            tt = work.tile([P, 2, 8, P], F32, name="tt", tag="tt", bufs=4)
+            o = work.tile([P, 8, P], F32, name="o", tag="o", bufs=4)
             def rope_products(n):
                 nc.vector.scalar_tensor_tensor(out=tt[:, :, n, :], in0=accs[u][n // 4][:, (n % 4) * P:(n % 4 + 1) * P].unsqueeze(1).to_broadcast([P, 2, P]),
                                                scalar=rstds[u][:, n:n + 1], in1=tables[which], op0=ALU.mult, op1=ALU.mult)
 
-            pieces = len(cuts) - 1
             for n in range(pe_from, 8):
                 rope_products(n)
-            pa = tp_pool.tile([P, (8 - pe_from) * P], F32, name="tp", tag="tp")
-            nc.tensor.matmul(out=pa[:], lhsT=ident[:], rhs=tt[:, 0, pe_from:8].rearrange("p n d -> p (n d)"), start=True, stop=False)
-            nc.tensor.matmul(out=pa[:].rearrange("p (m e) -> p m e", e=2), lhsT=ident[:],
+            pa = banks.tile([P, GROUP], F32, name="bank", tag="bank")
+            cols = (8 - pe_from) * P
+            nc.tensor.matmul(out=pa[:, 0:cols], lhsT=ident[:], rhs=tt[:, 0, pe_from:8].rearrange("p n d -> p (n d)"), start=True, stop=False)
+            nc.tensor.matmul(out=pa[:, 0:cols].rearrange("p (m e) -> p m e", e=2), lhsT=ident[:],
                              rhs=tt[:, 1, pe_from:8].rearrange("p n (j e) -> p (n j) e", e=2)[:, :, ::-1], start=False, stop=True)
-            nc.scalar.copy(out=o[:, pe_from:8].rearrange("p n d -> p (n d)"), in_=pa[:])
+            nc.scalar.copy(out=o[:, pe_from:8].rearrange("p n d -> p (n d)"), in_=pa[:, 0:cols])
             for n0, n1 in zip(cuts[:-1], cuts[1:]):
                 for n in range(n0, n1):
                     if n == pe_from - 1 and before_last is not None:
                         before_last()
                     rope_products(n)
+                eng = nc.gpsimd if n0 < own_from else nc.vector
                 eng.tensor_tensor(out=o[:, n0:n1].rearrange("p n (j e) -> p (n j) e", e=2),
                                   in0=tt[:, 0, n0:n1].rearrange("p n (j e) -> p (n j) e", e=2),
                                   in1=tt[:, 1, n0:n1].rearrange("p n (j e) -> p (n j) e", e=2)[:, :, ::-1], op=ALU.add)
-                if pieces > 1:
+                if store_each:
                     nc.sync.dma_start(out=outs[which][w, n0:n1].rearrange("n h d -> h n d"), in_=o[:, n0:n1])
                     if n0 == 0:
                         nc.sync.dma_start(out=outs[which][w, pe_from:8].rearrange("n h d -> h n d"), in_=o[:, pe_from:8])
-            if pieces == 1:
+            if not store_each:
                 nc.sync.dma_start(out=outs[which][w].rearrange("n h d -> h n d"), in_=o[:])
 
         tiles = [(c, a) for c in order for a in range(4)]
@@ -250,9 +248,11 @@ def tile_seisdit_pa_kernel(tc, x, w_qkv_bytes, w_qkv_scale, q_norm_w, k_norm_w, 
                 unit_tail(u, PE_FROM, [0, PE_FROM], lambda: quantize_w(order[-1]))
             elif u + 3 < 2 * NW:
                 unit_tail(u, PE_FROM, [0, PE_FROM])
-            elif u < 2 * NW - 1:
+            elif u < 2 * NW - 2:
                 unit_tail(u, PE_FROM_END, [0, PE_FROM_END])
+            elif u < 2 * NW - 1:
+                unit_tail(u, PE_FROM_END, [0, 3, PE_FROM_END])
             else:
-                unit_tail(u, PE_FROM_END, [0, 2, 4, PE_FROM_END])
+                unit_tail(u, 6, [0, 2, 4, 6], own_from=4, store_each=True)
             if u + 3 < 2 * NW:
                 unit_head(u + 3)

@@ -39,8 +39,8 @@ def tile_seisdit_pa_kernel(tc, x, w_qkv_bytes, w_qkv_scale, q_norm_w, k_norm_w, 
         banks = ctx.enter_context(tc.psum_pool(name="banks", bufs=8))
         ctx.enter_context(tc.manual_schedule())
 
-        sc = keep.tile([P, C], F32, name="sc")
-        nc.sync.dma_start(out=sc[:], in_=w_qkv_scale.rearrange("o k -> (o k)").partition_broadcast(P))
+        sc_col = keep.tile([P, 2, 4], F32, name="sc_col")
+        nc.sync.dma_start(out=sc_col[:], in_=w_qkv_scale.rearrange("o (g p t) -> p (o g) t", p=P, t=4))
         wb = {}
         for c in order:
             wb[c] = keep.tile([P, 4, C], U8, name="wbytes%d" % c)
@@ -93,6 +93,16 @@ def tile_seisdit_pa_kernel(tc, x, w_qkv_bytes, w_qkv_scale, q_norm_w, k_norm_w, 
         nc.vector.scalar_tensor_tensor(out=r1[:], in0=turns[:], scalar=-TWO_PI_HI, in1=ang[:], op0=ALU.mult, op1=ALU.add)
         red = keep.tile([P, 64], F32, name="red")
         nc.vector.scalar_tensor_tensor(out=red[:], in0=turns[:], scalar=-TWO_PI_LO, in1=r1[:], op0=ALU.mult, op1=ALU.add)
+        sc = keep.tile([P, C], F32, name="sc")
+        for g in range(2):
+            spread = banks.tile([P, 4, P], F32, name="bank", tag="bank")
+            for t in range(4):
+                nc.tensor.transpose(spread[:, t, :], sc_col[:, g, t:t + 1].to_broadcast([P, P]), ident[:])
+            half = sc[:, g * GROUP:(g + 1) * GROUP].rearrange("p (r t) -> p r t", t=4)
+            if g == 0:
+                nc.scalar.copy(out=half, in_=spread[:].rearrange("p t r -> p r t"))
+            else:
+                nc.vector.tensor_copy(out=half, in_=spread[:].rearrange("p t r -> p r t"))
         sh = keep.tile([P, 64], F32, name="sh")
         nc.scalar.activation(out=sh[:], in_=red[:], func=ACT.Sin, scale=0.5)
         ab = keep.tile([P, 64], F32, name="ab")

@@ -99,10 +99,7 @@ def tile_seisdit_pa_kernel(tc, x, w_qkv_bytes, w_qkv_scale, q_norm_w, k_norm_w, 
             for t in range(4):
                 nc.tensor.transpose(spread[:, t, :], sc_col[:, g, t:t + 1].to_broadcast([P, P]), ident[:])
             half = sc[:, g * GROUP:(g + 1) * GROUP].rearrange("p (r t) -> p r t", t=4)
-            if g == 0:
-                nc.scalar.copy(out=half, in_=spread[:].rearrange("p t r -> p r t"))
-            else:
-                nc.vector.tensor_copy(out=half, in_=spread[:].rearrange("p t r -> p r t"))
+            nc.scalar.copy(out=half, in_=spread[:].rearrange("p t r -> p r t"))
         sh = keep.tile([P, 64], F32, name="sh")
         nc.scalar.activation(out=sh[:], in_=red[:], func=ACT.Sin, scale=0.5)
         ab = keep.tile([P, 64], F32, name="ab")
@@ -142,7 +139,10 @@ def tile_seisdit_pa_kernel(tc, x, w_qkv_bytes, w_qkv_scale, q_norm_w, k_norm_w, 
             if a == 0:
                 gw_of[c] = work.tile([P, 4096], BF16, name="gw", tag="gw", bufs=4, align_bytes=64)
             wbf = work.tile([P, C], BF16, name="wbf", tag="wbf", bufs=8)
-            nc.vector.tensor_tensor(out=wbf[:], in0=wb[c][:, a, :].bitcast(FP8), in1=sc[:], op=ALU.mult)
+            n_parts = 2 if (c, a) == (order[0], 0) else 1
+            for part in range(n_parts):
+                ks = slice(part * C // n_parts, (part + 1) * C // n_parts)
+                nc.vector.tensor_tensor(out=wbf[:, ks], in0=wb[c][:, a, ks].bitcast(FP8), in1=sc[:, ks], op=ALU.mult)
             dst = gw_of[c][:].bitcast(F32).rearrange("p (g r u) -> p g r u", g=2, u=2)[:, :, a * P:(a + 1) * P, :]
             turn(wbf[:].bitcast(F32), dst)
 
@@ -245,13 +245,12 @@ def tile_seisdit_pa_kernel(tc, x, w_qkv_bytes, w_qkv_scale, q_norm_w, k_norm_w, 
                 build_tables()
             if a == 2 and t > 2:
                 quantize_w(tiles[t - 3][0])
-            if t >= 7 and t % 2 == 1 and nv < len(values):
+            if 7 <= t < 18 and t % 2 == 1:
                 value_bank(*values[nv])
                 value_bank(*values[nv + 1])
                 nv += 2
-            if t >= len(tiles) - 2:
-                unit_head(t - (len(tiles) - 2))
-        unit_head(2)
+            if t >= 19 and t % 2 == 1:
+                unit_head((t - 19) // 2)
 
         for u in range(2 * NW):
             if u == 0:
@@ -266,3 +265,6 @@ def tile_seisdit_pa_kernel(tc, x, w_qkv_bytes, w_qkv_scale, q_norm_w, k_norm_w, 
                 unit_tail(u, 6, [0, 2, 4, 6], own_from=4, store_each=True)
             if u + 3 < 2 * NW:
                 unit_head(u + 3)
+            if u % 2 == 1 and nv < len(values):
+                value_bank(*values[nv])
+                nv += 1

@@ -245,10 +245,9 @@ def tile_seisdit_pa_kernel(tc, x, w_qkv_bytes, w_qkv_scale, q_norm_w, k_norm_w, 
                 build_tables()
             if a == 2 and t > 2:
                 quantize_w(tiles[t - 3][0])
-            if 7 <= t < 18 and t % 2 == 1:
+            for i in range({7: 2, 9: 2, 11: 2, 13: 3, 15: 3, 17: 2}.get(t, 0)):
                 value_bank(*values[nv])
-                value_bank(*values[nv + 1])
-                nv += 2
+                nv += 1
             if t >= 19 and t % 2 == 1:
                 unit_head((t - 19) // 2)
 
@@ -256,11 +255,14 @@ def tile_seisdit_pa_kernel(tc, x, w_qkv_bytes, w_qkv_scale, q_norm_w, k_norm_w, 
             if u == 0:
                 unit_tail(u, PE_FROM, [0, PE_FROM], lambda: quantize_w(order[-1]))
             elif u + 3 < 2 * NW:
-                unit_tail(u, PE_FROM, [0, PE_FROM])
+                if u >= 10:
+                    unit_tail(u, PE_FROM, [0, 4, PE_FROM], store_each=True)
+                else:
+                    unit_tail(u, PE_FROM, [0, PE_FROM])
             elif u < 2 * NW - 2:
-                unit_tail(u, PE_FROM_END, [0, PE_FROM_END])
+                unit_tail(u, PE_FROM_END, [0, 3, PE_FROM_END], store_each=True)
             elif u < 2 * NW - 1:
-                unit_tail(u, PE_FROM_END, [0, 3, PE_FROM_END])
+                unit_tail(u, PE_FROM_END, [0, 3, PE_FROM_END], store_each=True)
             else:
                 unit_tail(u, 6, [0, 2, 4, 6], own_from=4, store_each=True)
             if u + 3 < 2 * NW:

from contextlib import ExitStack

import concourse.mybir as mybir
from concourse.masks import make_identity

FLOPS = 2 * 1024 * 1024 * 3072

F32 = mybir.dt.float32
BF16 = mybir.dt.bfloat16
U32 = mybir.dt.uint32
U8 = mybir.dt.uint8
I32 = mybir.dt.int32
FP8 = mybir.dt.float8_e4m3fn
FP8X4 = mybir.dt.float8_e4m3fn_x4
ALU = mybir.AluOpType
ACT = mybir.ActivationFunctionType

P = 128
NW = 8
C = 1024
GROUP = 512
EPS = 1e-6
PI = 3.141592653589793
E = 2.718281828459045
TWO_PI_HI = 6.28125
TWO_PI_LO = 2.0 * PI - TWO_PI_HI
PE_FROM = 7
PE_FROM_END = 5


def tile_seisdit_pa_kernel(tc, x, w_qkv_bytes, w_qkv_scale, q_norm_w, k_norm_w, out_0, out_1, out_2):
    nc = tc.nc
    outs = (out_0, out_1, out_2)
    order = [4, 5, 0, 1, 2, 3]

    with ExitStack() as ctx:
        keep = ctx.enter_context(tc.tile_pool(name="keep", bufs=1))
        work = ctx.enter_context(tc.tile_pool(name="work", bufs=2))
        banks = ctx.enter_context(tc.psum_pool(name="banks", bufs=8))
        ctx.enter_context(tc.manual_schedule())

        sc_col = keep.tile([P, 2, 4], F32, name="sc_col")
        nc.sync.dma_start(out=sc_col[:], in_=w_qkv_scale.rearrange("o (g p t) -> p (o g) t", p=P, t=4))
        wb = {}
        for c in order:
            wb[c] = keep.tile([P, 4, C], U8, name="wbytes%d" % c)
        x_sb = []
        for i in range(4):
            x_sb.append(keep.tile([P, 2, C], BF16, name="x_sb%d" % i))

        def load_w(c, a0, a1):
            rows = w_qkv_bytes[c * GROUP + a0 * P:c * GROUP + a1 * P, :]
            nc.sync.dma_start(out=wb[c][:, a0:a1, :], in_=rows.rearrange("(a p) k -> p a k", p=P))

        def load_x(i):
            nc.sync.dma_start(out=x_sb[i][:], in_=x[0, :, 2 * i:2 * i + 2, :])

        load_w(order[0], 0, 1)
        load_w(order[0], 1, 2)
        load_x(0)
        load_w(order[0], 2, 4)
        load_x(1)
        load_w(order[1], 0, 2)
        load_x(2)
        load_w(order[1], 2, 4)
        load_x(3)
        gains = keep.tile([P, 2, P], BF16, name="gains")
        for i, gvec in enumerate((q_norm_w, k_norm_w)):
            nc.sync.dma_start(out=gains[:, i, :], in_=gvec.partition_broadcast(P))
        for c in order[2:]:
            load_w(c, 0, 4)

        h_i = keep.tile([P, 1], I32, name="h_i")
        nc.gpsimd.iota(h_i[:], pattern=[[0, 1]], base=0, channel_multiplier=1)
        ident = keep.tile([P, P], F32, name="ident")
        make_identity(nc, ident[:])
        fr = keep.tile([P, 64], F32, name="fr")
        nc.vector.memset(fr[:, 0:1], 1.0)
        warm = keep.tile([P, 2], F32, name="warm")
        nc.scalar.activation(out=warm[:, 0:1], in_=fr[:, 0:1], func=ACT.Sin)
        for b in range(6):
            n = 1 << b
            nc.vector.tensor_scalar(out=fr[:, n:2 * n], in0=fr[:, 0:n], scalar1=E ** (12.0 * n / 63.0), scalar2=None, op0=ALU.mult)
        h_f = keep.tile([P, 1], F32, name="h_f")
        nc.vector.tensor_copy(out=h_f[:], in_=h_i[:])
        ang = keep.tile([P, 64], F32, name="ang")
        nc.vector.tensor_scalar(out=ang[:], in0=fr[:], scalar1=h_f[:, 0:1], scalar2=(128.0 / 127.0) * E ** (-12.0), op0=ALU.mult, op1=ALU.mult)
        turns_i = keep.tile([P, 64], I32, name="turns_i")
        nc.vector.tensor_scalar(out=turns_i[:], in0=ang[:], scalar1=1.0 / (2.0 * PI), scalar2=None, op0=ALU.mult)
        turns = keep.tile([P, 64], F32, name="turns")
        nc.vector.tensor_copy(out=turns[:], in_=turns_i[:])
        r1 = keep.tile([P, 64], F32, name="r1")
        nc.vector.scalar_tensor_tensor(out=r1[:], in0=turns[:], scalar=-TWO_PI_HI, in1=ang[:], op0=ALU.mult, op1=ALU.add)
        red = keep.tile([P, 64], F32, name="red")
        nc.vector.scalar_tensor_tensor(out=red[:], in0=turns[:], scalar=-TWO_PI_LO, in1=r1[:], op0=ALU.mult, op1=ALU.add)
        sc = keep.tile([P, C], F32, name="sc")
        for g in range(2):
            spread = banks.tile([P, 4, P], F32, name="bank", tag="bank")
            for t in range(4):
                nc.tensor.transpose(spread[:, t, :], sc_col[:, g, t:t + 1].to_broadcast([P, P]), ident[:])
            half = sc[:, g * GROUP:(g + 1) * GROUP].rearrange("p (r t) -> p r t", t=4)
            nc.scalar.copy(out=half, in_=spread[:].rearrange("p t r -> p r t"))
        sh = keep.tile([P, 64], F32, name="sh")
        nc.scalar.activation(out=sh[:], in_=red[:], func=ACT.Sin, scale=0.5)
        ab = keep.tile([P, 64], F32, name="ab")
        nc.scalar.activation(out=ab[:], in_=red[:], func=ACT.Abs)
        ch = keep.tile([P, 64], F32, name="ch")
        nc.scalar.activation(out=ch[:], in_=ab[:], func=ACT.Sin, scale=-0.5, bias=PI / 2.0)
        sq = keep.tile([P, 64], F32, name="sq")
        nc.scalar.activation(out=sq[:], in_=sh[:], func=ACT.Square)
        trig = keep.tile([P, 2, 64, 2], F32, name="trig")
        nc.scalar.activation(out=trig[:, 0], in_=sq[:].unsqueeze(2).to_broadcast([P, 64, 2]), func=ACT.Copy, scale=-2.0, bias=1.0)
        nc.scalar.activation(out=warm[:, 1:2], in_=fr[:, 0:1], func=ACT.Abs_reciprocal_sqrt)
        tables_all = keep.tile([P, 2, 2, P], F32, name="tables")
        tables = [tables_all[:, 0], tables_all[:, 1]]

        def build_tables():
            nc.vector.scalar_tensor_tensor(out=trig[:, 1, :, 0], in0=sh[:], scalar=2.0, in1=ch[:], op0=ALU.mult, op1=ALU.mult)
            nc.vector.scalar_tensor_tensor(out=trig[:, 1, :, 1], in0=sh[:], scalar=-2.0, in1=ch[:], op0=ALU.mult, op1=ALU.mult)
            nc.vector.tensor_tensor(out=tables_all[:], in0=gains[:].unsqueeze(2).to_broadcast([P, 2, 2, P]),
                                    in1=trig[:].rearrange("p a j e -> p a (j e)").unsqueeze(1).to_broadcast([P, 2, 2, P]), op=ALU.mult)

        def turn_only(words):
            tp = banks.tile([P, 2, 2, P], F32, name="bank", tag="bank")
            for g in range(2):
                for u in range(2):
                    nc.tensor.transpose(tp[:, g, u, :], words[:, 256 * g + u:256 * (g + 1):2], ident[:])
            return tp

        def turn(words, dst):
            tp = turn_only(words)
            nc.scalar.copy(out=dst, in_=tp[:].rearrange("p g u r -> p g r u"))

        gw_of = {}
        wc = {}
        ws = {}

        def widen_and_turn(c, a):
            if a == 0:
                gw_of[c] = work.tile([P, 4096], BF16, name="gw", tag="gw", bufs=4, align_bytes=64)
            wbf = work.tile([P, C], BF16, name="wbf", tag="wbf", bufs=8)
            n_parts = 2 if (c, a) == (order[0], 0) else 1
            for part in range(n_parts):
                ks = slice(part * C // n_parts, (part + 1) * C // n_parts)
                nc.vector.tensor_tensor(out=wbf[:, ks], in0=wb[c][:, a, ks].bitcast(FP8), in1=sc[:, ks], op=ALU.mult)
            dst = gw_of[c][:].bitcast(F32).rearrange("p (g r u) -> p g r u", g=2, u=2)[:, :, a * P:(a + 1) * P, :]
            turn(wbf[:].bitcast(F32), dst)

        def quantize_w(c):
            wc[c] = keep.tile([P, 2, GROUP], U32, name="wc%d" % c, align_bytes=64)
            ws[c] = keep.tile([P, 2, GROUP], U8, name="ws%d" % c, align_bytes=64)
            nc.vector.quantize_mx(out=wc[c][:].rearrange("p g r -> p (g r)").bitcast(FP8X4), scales=ws[c][:].rearrange("p g r -> p (g r)"), in_=gw_of[c][:])

        xg_of = {}
        xc = {}
        xs = {}

        def turn_x(i, b):
            if b == 0:
                xg_of[i] = work.tile([P, 2 * C], BF16, name="xg", tag="xg", bufs=4, align_bytes=64)
            turn(x_sb[i][:, b, :].bitcast(F32), xg_of[i][:, b * C:(b + 1) * C].bitcast(F32).rearrange("p (g r u) -> p g r u", g=2, u=2))

        def quantize_x(i):
            codes = keep.tile([P, 512], U32, name="xc%d" % i, align_bytes=64)
            planes = keep.tile([P, 512], U8, name="xs%d" % i, align_bytes=64)
            nc.vector.quantize_mx(out=codes[:].bitcast(FP8X4), scales=planes[:], in_=xg_of[i][:])
            for b in range(2):
                xc[2 * i + b] = codes[:, b * 256:(b + 1) * 256]
                xs[2 * i + b] = planes[:, b * 256:(b + 1) * 256]

        def product(c, w, late=False):
            if late:
                acc = banks.tile([P, GROUP], F32, name="bank", tag="bank")
            else:
                acc = banks.tile([P, GROUP], F32, name="bank", tag="bank")
            for g in range(2):
                cols = slice(g * P, (g + 1) * P)
                nc.tensor.matmul_mx(out=acc[:], lhsT=xc[w][:, cols].bitcast(FP8X4), lhsT_scale=xs[w][:, cols],
                                    rhs=wc[c][:, g, :].bitcast(FP8X4), rhs_scale=ws[c][:, g, :],
                                    start=(g == 0), stop=(g == 1))
            return acc

        def value_bank(c, w, late=False):
            acc = product(c, w, late)
            ov = work.tile([P, 4, P], F32, name="ov", tag="ov", bufs=6)
            nc.scalar.copy(out=ov[:].rearrange("p n d -> p (n d)"), in_=acc[:])
            n0 = 4 * (c % 2)
            nc.sync.dma_start(out=outs[2][w, n0:n0 + 4].rearrange("n h d -> h n d"), in_=ov[:])

        accs = {}
        rstds = {}

        def unit_head(u):
            which, w = u // NW, u % NW
            accs[u] = [product(2 * which + b, w) for b in range(2)]
            ss = work.tile([P, 8], F32, name="ss", tag="ss", bufs=4)
            for n in range(8):
                junk = work.tile([P, P], BF16, name="junk", tag="junk", bufs=2)
                nc.scalar.activation(out=junk[:], in_=accs[u][n // 4][:, (n % 4) * P:(n % 4 + 1) * P], func=ACT.Square, accum_out=ss[:, n:n + 1])
            rstds[u] = work.tile([P, 8], F32, name="rstd", tag="rstd", bufs=4)
            nc.scalar.activation(out=rstds[u][:], in_=ss[:], func=ACT.Abs_reciprocal_sqrt, scale=1.0 / 128.0, bias=EPS)

        def unit_tail(u, pe_from, cuts, before_last=None, own_from=8, store_each=False):
            which, w = u // NW, u % NW
            tt = work.tile([P, 2, 8, P], F32, name="tt", tag="tt", bufs=4)
            o = work.tile([P, 8, P], F32, name="o", tag="o", bufs=4)
            def rope_products(n):
                nc.vector.scalar_tensor_tensor(out=tt[:, :, n, :], in0=accs[u][n // 4][:, (n % 4) * P:(n % 4 + 1) * P].unsqueeze(1).to_broadcast([P, 2, P]),
                                               scalar=rstds[u][:, n:n + 1], in1=tables[which], op0=ALU.mult, op1=ALU.mult)

            for n in range(pe_from, 8):
                rope_products(n)
            pa = banks.tile([P, GROUP], F32, name="bank", tag="bank")
            cols = (8 - pe_from) * P
            nc.tensor.matmul(out=pa[:, 0:cols], lhsT=ident[:], rhs=tt[:, 0, pe_from:8].rearrange("p n d -> p (n d)"), start=True, stop=False)
            nc.tensor.matmul(out=pa[:, 0:cols].rearrange("p (m e) -> p m e", e=2), lhsT=ident[:],
                             rhs=tt[:, 1, pe_from:8].rearrange("p n (j e) -> p (n j) e", e=2)[:, :, ::-1], start=False, stop=True)
            nc.scalar.copy(out=o[:, pe_from:8].rearrange("p n d -> p (n d)"), in_=pa[:, 0:cols])
            for n0, n1 in zip(cuts[:-1], cuts[1:]):
                for n in range(n0, n1):
                    if n == pe_from - 1 and before_last is not None:
                        before_last()
                    rope_products(n)
                eng = nc.gpsimd if n0 < own_from else nc.vector
                eng.tensor_tensor(out=o[:, n0:n1].rearrange("p n (j e) -> p (n j) e", e=2),
                                  in0=tt[:, 0, n0:n1].rearrange("p n (j e) -> p (n j) e", e=2),
                                  in1=tt[:, 1, n0:n1].rearrange("p n (j e) -> p (n j) e", e=2)[:, :, ::-1], op=ALU.add)
                if store_each:
                    nc.sync.dma_start(out=outs[which][w, n0:n1].rearrange("n h d -> h n d"), in_=o[:, n0:n1])
                    if n0 == 0:
                        nc.sync.dma_start(out=outs[which][w, pe_from:8].rearrange("n h d -> h n d"), in_=o[:, pe_from:8])
            if not store_each:
                nc.sync.dma_start(out=outs[which][w].rearrange("n h d -> h n d"), in_=o[:])

        tiles = [(c, a) for c in order for a in range(4)]
        values = [(c, w) for c in (4, 5) for w in range(NW)]
        nv = 0
        for t, (c, a) in enumerate(tiles):
            widen_and_turn(c, a)
            if t < 8:
                turn_x(t // 2, t % 2)
            if t in (5, 7, 9, 11):
                quantize_x((t - 5) // 2)
            if t == 8:
                build_tables()
            if a == 2 and t > 2:
                quantize_w(tiles[t - 3][0])
            for i in range({7: 2, 9: 2, 11: 2, 13: 3, 15: 3, 17: 2}.get(t, 0)):
                value_bank(*values[nv])
                nv += 1
            if t >= 19 and t % 2 == 1:
                unit_head((t - 19) // 2)

        for u in range(2 * NW):
            if u == 0:
                unit_tail(u, PE_FROM, [0, PE_FROM], lambda: quantize_w(order[-1]))
            elif u + 3 < 2 * NW:
                if u >= 10:
                    unit_tail(u, PE_FROM, [0, 4, PE_FROM], store_each=True)
                else:
                    unit_tail(u, PE_FROM, [0, PE_FROM])
            elif u < 2 * NW - 2:
                unit_tail(u, PE_FROM_END, [0, 3, PE_FROM_END], store_each=True)
            elif u < 2 * NW - 1:
                unit_tail(u, PE_FROM_END, [0, 3, PE_FROM_END], store_each=True)
            else:
                unit_tail(u, 6, [0, 2, 4, 6], own_from=4, store_each=True)
            if u + 3 < 2 * NW:
                unit_head(u + 3)
            if u % 2 == 1 and nv < len(values):
                value_bank(*values[nv])
                nv += 1
